import numpy as np
import ml_dtypes


def mxq(x, axis, fmt="e4m3"):
    dtype, down = {"e4m3": (ml_dtypes.float8_e4m3fn, 7), "e5m2": (ml_dtypes.float8_e5m2, 14)}[fmt]
    v = np.moveaxis(np.asarray(x, np.float32).astype(ml_dtypes.bfloat16).astype(np.float64), axis, -1)
    blocks = v.reshape(v.shape[:-1] + (-1, 32))
    amax = np.abs(blocks).max(-1, keepdims=True)
    byte = np.maximum(np.where(amax > 0, np.frexp(amax)[1] - 1 + 127, 0) - down, 1)
    scale = np.exp2(byte - 127.0)
    codes = (blocks / scale).astype(np.float32).astype(dtype).astype(np.float64)
    return np.moveaxis((codes * scale).reshape(v.shape), -1, axis)


WIDE = False


def mx_kscale(k):
    if not WIDE:
        return np.ones(k)
    levels = np.array([10, -10, 5, -5, 0])
    if k % 512:
        return np.exp2(np.random.permutation(np.resize(levels, k // 32))).repeat(32)
    a = np.empty((k // 512, 16))
    for p in range(k // 512):
        a[p, :8] = np.random.permutation(np.resize(levels, 8))
        for g in range(8):
            far = levels[np.abs(levels - a[p, g]) >= 10]
            a[p, g + 8] = far[np.random.randint(len(far))]
    return np.exp2(a.ravel()).repeat(32)


BF16 = ml_dtypes.bfloat16


def bf(x):
    return np.asarray(x, np.float32).astype(BF16)


def f64(x):
    return np.asarray(x).astype(np.float64)


B, S, H, HD, LAT = 2, 2048, 4, 128, 512
HID = H * HD
ROT = HD // 2
HALF = ROT // 2
BASE = 10000.0


def make_rotary():
    inv_freq = 1.0 / BASE ** (np.arange(0, ROT, 2) / ROT)
    ang = np.arange(S)[:, None] * inv_freq[None, :]
    return np.concatenate([np.sin(ang), np.cos(ang)], axis=-1)[None, None, :, :]


def apply_rope(x, emb):
    x1, x2 = x[..., :HALF], x[..., HALF:]
    sin = emb[..., :HALF].transpose(0, 2, 1, 3)
    cos = emb[..., HALF:].transpose(0, 2, 1, 3)
    return np.concatenate([x1 * cos - x2 * sin, x1 * sin + x2 * cos], axis=-1)


def draw0():
    s, t = mx_kscale(HID), mx_kscale(LAT)
    return {"hidden_states": bf(np.random.standard_normal((B, S, HID)) * s),
            "rotary_emb": bf(make_rotary()),
            "W_kv_d": bf(np.random.standard_normal((HID, LAT)) / np.sqrt(HID) / s[:, None] * t),
            "W_k_u": bf(np.random.standard_normal((LAT, H * ROT)) / np.sqrt(LAT) / t[:, None]),
            "W_v_u": bf(np.random.standard_normal((LAT, H * HD)) / np.sqrt(LAT) / t[:, None]),
            "W_rope_k": bf(np.random.standard_normal((HID, H * ROT)) / np.sqrt(HID) / s[:, None])}


def core(hidden_states, rotary_emb, W_kv_d, W_k_u, W_v_u, W_rope_k):
    emb = f64(rotary_emb)
    xq = mxq(f64(hidden_states), 2, "e4m3")
    kv_d = xq @ mxq(f64(W_kv_d), 0, "e4m3")
    kvq = mxq(kv_d, 2, "e4m3")
    k_c = (kvq @ mxq(f64(W_k_u), 0, "e4m3")).reshape(B, S, H, ROT)
    v = (kvq @ mxq(f64(W_v_u), 0, "e4m3")).reshape(B, S, H, HD)
    k_r = (xq @ mxq(f64(W_rope_k), 0, "e4m3")).reshape(B, S, H, ROT)
    k_r = apply_rope(k_r, emb)
    k = np.concatenate([k_c, k_r], axis=-1)
    return k, v


def e4m3fn_bytes(y):
    return np.clip(np.asarray(y, np.float64), -448.0, 448.0).astype(np.float32).astype(ml_dtypes.float8_e4m3fn).view(np.uint8)


def e4m3fn_values(b):
    return np.asarray(b, np.uint8).view(ml_dtypes.float8_e4m3fn).astype(np.float64)


def setup_inputs():
    d = draw0()
    x0 = np.asarray(d['hidden_states']).astype(np.float64)
    s = (np.max(np.abs(x0), axis=(0, 1), keepdims=True) / 448.0).astype(np.float32)
    out = {}
    for k, v in d.items():
        if k == 'hidden_states':
            out['hidden_states_bytes'] = e4m3fn_bytes(x0 / s.astype(np.float64))
            out['hidden_states_scale'] = s
        else:
            out[k] = v
    return out


def reference(hidden_states_bytes, hidden_states_scale, rotary_emb, W_kv_d, W_k_u, W_v_u, W_rope_k):
    return core(e4m3fn_values(hidden_states_bytes) * hidden_states_scale.astype(np.float64), rotary_emb, W_kv_d, W_k_u, W_v_u, W_rope_k)

@@ -1,0 +1,269 @@
+from contextlib import ExitStack
+
+import concourse.mybir as mybir
+from concourse.masks import make_identity
+
+F32 = mybir.dt.float32
+BF16 = mybir.dt.bfloat16
+U32 = mybir.dt.uint32
+U8 = mybir.dt.uint8
+FP8 = mybir.dt.float8_e4m3fn
+FP8X4 = mybir.dt.float8_e4m3fn_x4
+MULT = mybir.AluOpType.mult
+ADD = mybir.AluOpType.add
+SUB = mybir.AluOpType.subtract
+
+P = 128
+B, S, HID, LAT = 2, 2048, 512, 512
+H, HD, ROT, HALF = 4, 128, 64, 32
+GROUP = 4 * P
+STEP = 2 * P
+STEPS = B * S // STEP
+
+FLOPS = 2 * B * S * 512 * (512 + 256 + 512 + 256)
+
+
+def tile_llamaattention_pb_t_kernel(
+    tc, x_bytes, x_scale, rotary, w_kv_d, w_k_u, w_v_u, w_rope, k_out, v_out
+):
+    nc = tc.nc
+    x_view = x_bytes.rearrange("b (g p j) k -> b g p j k", p=P, j=4)
+    k_view = k_out.rearrange("b (g p j) h d -> b g p j (h d)", p=P, j=4)
+    v_view = v_out.rearrange("b (g p j) h d -> b g p j (h d)", p=P, j=4)
+
+    with ExitStack() as ctx:
+        const = ctx.enter_context(tc.tile_pool(name="const", bufs=1))
+        stage = ctx.enter_context(tc.tile_pool(name="stage", bufs=3))
+        outs = ctx.enter_context(tc.tile_pool(name="outs", bufs=4))
+        psum = ctx.enter_context(tc.psum_pool(name="psum", bufs=8))
+        ctx.enter_context(tc.manual_schedule())
+
+        ident = const.tile([P, P], F32)
+        make_identity(nc, ident[:])
+
+        xb = []
+        for g in range(8):
+            xbytes = const.tile([P, 4, 512], U8, name="xbytes%d" % g)
+            xb.append(xbytes)
+        scale = const.tile([P, 4], F32)
+        wd_raw = const.tile([P, 4, 512], BF16)
+        wr_raw = const.tile([P, 4, 256], BF16)
+        wk_raw = const.tile([P, 4, 256], BF16)
+        wv_raw = const.tile([P, 4, 512], BF16)
+        rot = const.tile([P, 4, 4, ROT], BF16)
+
+        nc.sync.dma_start(out=xb[0][:, 0:2, :], in_=x_view[0, 0][:, 0:2, :])
+        nc.sync.dma_start(out=scale[:], in_=x_scale.rearrange("a o (p t) -> (a o p) t", t=4))
+        nc.sync.dma_start(out=wd_raw[:], in_=w_kv_d.rearrange("(p j) c -> p j c", j=4))
+        nc.sync.dma_start(out=xb[0][:, 2:4, :], in_=x_view[0, 0][:, 2:4, :])
+        nc.sync.dma_start(out=wr_raw[:], in_=w_rope.rearrange("(p j) c -> p j c", j=4))
+        nc.sync.dma_start(out=rot[:], in_=rotary.rearrange("a o (g p j) f -> (a o p) g j f", p=P, j=4))
+        nc.sync.dma_start(out=wk_raw[:], in_=w_k_u.rearrange("(p j) c -> p j c", j=4))
+        nc.sync.dma_start(out=wv_raw[:], in_=w_v_u.rearrange("(p j) c -> p j c", j=4))
+        for g in range(1, 8):
+            nc.sync.dma_start(out=xb[g][:], in_=x_view[g // 4, g % 4])
+
+        xw, xg, xq, xs = {}, {}, {}, {}
+        kg, kq, ks = {}, {}, {}
+        banks = {}
+        prod, kt, vt = {}, {}, {}
+
+        def cast(s, engines):
+            wide = stage.tile([P, 2, 512], BF16, bufs=5, name="wide")
+            for a in range(2):
+                src = xb[s // 2][:, 2 * (s % 2) + a, :].bitcast(FP8)
+                if engines[a] == "v":
+                    nc.vector.tensor_copy(out=wide[:, a, :], in_=src)
+                else:
+                    nc.gpsimd.tensor_copy(out=wide[:, a, :], in_=src)
+            xw[s] = wide
+
+        def transposes(s):
+            bank = psum.tile([P, 512], F32, name="bank")
+            halves = bank[:].rearrange("p (u a m) -> p u a m", u=2, a=2)
+            words = xw.pop(s)[:].rearrange("p a k -> p (a k)").bitcast(F32)
+            for a in range(2):
+                for u in range(2):
+                    nc.tensor.transpose(halves[:, u, a, :], words[:, 256 * a + u : 256 * (a + 1) : 2], ident[:])
+            banks["t", s] = bank
+
+        def scaled(s):
+            bank = banks.pop(("t", s))
+            grouped = stage.tile([P, STEP, 2, 2], BF16, align_bytes=64, name="xgrouped")
+            nc.vector.tensor_tensor(
+                out=grouped[:],
+                in0=bank[:].bitcast(BF16).rearrange("p (u r e) -> p r u e", u=2, e=2),
+                in1=scale[:].rearrange("p (u e) -> p u e", e=2).unsqueeze(1).broadcast_to([P, STEP, 2, 2]),
+                op=MULT,
+            )
+            xg[s] = grouped
+
+        def quantize(src, width, pool, label, bufs):
+            codes = pool.tile([P, width], U32, align_bytes=64, bufs=bufs, name="%scodes" % label)
+            scales = pool.tile([P, width], U8, align_bytes=64, bufs=bufs, name="%sscales" % label)
+            nc.vector.quantize_mx(out=codes[:].bitcast(FP8X4), scales=scales[:], in_=src)
+            return codes, scales
+
+        def quant_x(s):
+            xq[s], xs[s] = quantize(xg.pop(s)[:].rearrange("p r u e -> p (r u e)"), STEP, stage, "x", 3)
+
+        def mm(out, lhs, lhs_s, lc, rhs, rhs_s, rc, start=True, stop=True):
+            nc.tensor.matmul_mx(
+                out=out,
+                lhsT=lhs[:, lc].bitcast(FP8X4),
+                lhsT_scale=lhs_s[:, lc],
+                rhs=rhs[:, rc].bitcast(FP8X4),
+                rhs_scale=rhs_s[:, rc],
+                start=start,
+                stop=stop,
+            )
+
+        def latents(s):
+            for a in range(2):
+                bank = psum.tile([P, 512], F32, name="bank")
+                for t in range(4):
+                    cols = slice(128 * t, 128 * (t + 1))
+                    mm(bank[:, cols], wd_q, wd_s, cols, xq[s], xs[s], slice(128 * a, 128 * (a + 1)))
+                banks["d", s, a] = bank
+
+        def latent_copies(s):
+            grouped = stage.tile([P, 2, P, 4], BF16, align_bytes=64, name="kgrouped")
+            for a in range(2):
+                bank = banks.pop(("d", s, a))
+                nc.scalar.copy(out=grouped[:, a], in_=bank[:].rearrange("p (t m) -> p m t", t=4))
+            kg[s] = grouped
+
+        def quant_latent(s):
+            kq[s], ks[s] = quantize(kg.pop(s)[:].rearrange("p a m t -> p (a m t)"), STEP, stage, "k", 3)
+
+        def rope_matmuls(s):
+            codes, scales = xq.pop(s), xs.pop(s)
+            for a in range(2):
+                bank = psum.tile([P, 512], F32, name="bank")
+                rows = slice(128 * a, 128 * (a + 1))
+                mm(bank[:, 0:128], codes, scales, rows, wr_q, wr_s, slice(0, 128), True, False)
+                mm(bank[:, 0:128], codes, scales, rows, wr_q, wr_s, slice(128, 256), False, True)
+                mm(bank[:, 128:384], codes, scales, rows, wr_q, wr_s, slice(0, 256))
+                banks["r", s, a] = bank
+
+        def rope_products(s):
+            p = stage.tile([P, 3, 2, H, HALF], F32, name="products")
+            for a in range(2):
+                slab = (2 * s + a) % 16
+                bank = banks.pop(("r", s, a))
+                nc.vector.tensor_tensor(
+                    out=p[:, :, a],
+                    in0=bank[:, 0:384].rearrange("p (c h f) -> p c h f", c=3, h=H),
+                    in1=table[:, slab].unsqueeze(2).broadcast_to([P, 3, H, HALF]),
+                    op=MULT,
+                )
+            prod[s] = p
+            keys = outs.tile([P, 2, H, HD], F32, name="keys")
+            kt[s] = keys
+
+        def rope_sums(s):
+            p = prod.pop(s)
+            nc.vector.tensor_tensor(
+                out=kt[s][:, :, :, ROT:HD].rearrange("p a h (c f) -> p c (a h) f", c=2),
+                in0=p[:, 0].rearrange("p a h f -> p (a h) f").unsqueeze(1).broadcast_to([P, 2, 2 * H, HALF]),
+                in1=p[:, 1:3].rearrange("p c a h f -> p c (a h) f"),
+                op=ADD,
+            )
+
+        def values(s):
+            codes, scales = kq.pop(s), ks.pop(s)
+            for a in range(2):
+                bank = psum.tile([P, 512], F32, name="bank")
+                mm(bank[:], codes, scales, slice(128 * a, 128 * (a + 1)), wv_q, wv_s, slice(0, 512))
+                banks["v", s, a] = bank
+            bank = psum.tile([P, 512], F32, name="bank")
+            for a in range(2):
+                mm(bank[:, 256 * a : 256 * (a + 1)], codes, scales, slice(128 * a, 128 * (a + 1)), wk_q, wk_s, slice(0, 256))
+            banks["c", s] = bank
+
+        def value_copies(s):
+            vals = outs.tile([P, 2, 512], F32, name="vals")
+            for a in range(2):
+                nc.scalar.copy(out=vals[:, a, :], in_=banks.pop(("v", s, a))[:])
+            nc.scalar.copy(
+                out=kt[s][:, :, :, 0:ROT].rearrange("p a h d -> p (a h) d"),
+                in_=banks.pop(("c", s))[:].rearrange("p (q d) -> p q d", d=ROT),
+            )
+            vt[s] = vals
+
+        def store(s):
+            b, g, j = s // 8, (s // 2) % 4, 2 * (s % 2)
+            nc.sync.dma_start(out=v_view[b, g][:, j : j + 2, :], in_=vt.pop(s)[:])
+            nc.sync.dma_start(out=k_view[b, g][:, j : j + 2, :], in_=kt.pop(s)[:].rearrange("p a h d -> p a (h d)"))
+
+        cast(0, "vv")
+        cast(1, "gg")
+        wd_g = const.tile([P, 4, P, 4], BF16, align_bytes=64)
+        wd_in = wd_raw[:].rearrange("p j (m t) -> p t m j", t=4)
+        wr_g = const.tile([P, 2, H, HALF, 4], BF16, align_bytes=64)
+        wr_in = wr_raw[:].rearrange("p j (h c f) -> p c h f j", h=H, c=2)
+        wk_g = const.tile([P, 256, 4], BF16, align_bytes=64)
+        wv_g = const.tile([P, 512, 4], BF16, align_bytes=64)
+        wv_in = wv_raw[:].rearrange("p j c -> p c j")
+        table = const.tile([P, 16, 3, HALF], F32)
+        rot_in = rot[:].rearrange("p g j f -> p (g j) f")
+
+        def tables(lo, hi):
+            sin, cos = rot_in[:, lo:hi, 0:HALF], rot_in[:, lo:hi, HALF:ROT]
+            nc.gpsimd.tensor_scalar(out=table[:, lo:hi, 0, :], in0=cos, scalar1=1.0, scalar2=0.0, op0=MULT, op1=ADD)
+            nc.gpsimd.tensor_scalar(out=table[:, lo:hi, 1, :], in0=cos, scalar1=-1.0, scalar2=0.0, op0=MULT, op1=ADD)
+            nc.gpsimd.tensor_tensor(out=table[:, lo:hi, 2, :], in0=sin, in1=cos, op=SUB)
+            nc.gpsimd.tensor_tensor(out=table[:, lo:hi, 1, :], in0=table[:, lo:hi, 1, :], in1=sin, op=SUB)
+
+        transposes(0)
+        scaled(0)
+        nc.scalar.copy(out=wd_g[:, 2:4], in_=wd_in[:, 2:4])
+        nc.vector.tensor_copy(out=wd_g[:, 0:2], in_=wd_in[:, 0:2])
+        quant_x(0)
+        tables(0, 4)
+        for c in range(2):
+            nc.scalar.copy(out=wr_g[:, c], in_=wr_in[:, 1 - c])
+        wd_q, wd_s = quantize(wd_g[:].rearrange("p t m j -> p (t m j)"), 512, const, "wd", 1)
+        nc.gpsimd.tensor_scalar(
+            out=wk_g[:], in0=wk_raw[:].rearrange("p j c -> p c j"), scalar1=1.0, scalar2=0.0, op0=MULT, op1=ADD
+        )
+        cast(2, "gg")
+
+        transposes(1)
+        latents(0)
+        scaled(1)
+        wr_q, wr_s = quantize(wr_g[:].rearrange("p c h f j -> p (c h f j)"), 256, const, "wr", 1)
+        rope_matmuls(0)
+        latent_copies(0)
+        quant_x(1)
+        nc.vector.tensor_copy(out=wv_g[:, 0:256], in_=wv_in[:, 0:256])
+        nc.scalar.copy(out=wv_g[:, 256:512], in_=wv_in[:, 256:512])
+        quant_latent(0)
+        wk_q, wk_s = quantize(wk_g[:].rearrange("p c j -> p (c j)"), 256, const, "wk", 1)
+        rope_products(0)
+        wv_q, wv_s = quantize(wv_g[:].rearrange("p c j -> p (c j)"), 512, const, "wv", 1)
+        rope_sums(0)
+        cast(3, "gg")
+        tables(4, 16)
+
+        for i in range(STEPS):
+            if i + 2 < STEPS:
+                transposes(i + 2)
+            if i + 1 < STEPS:
+                latents(i + 1)
+                rope_matmuls(i + 1)
+            values(i)
+            if i + 2 < STEPS:
+                scaled(i + 2)
+            if i + 1 < STEPS:
+                latent_copies(i + 1)
+                rope_products(i + 1)
+            value_copies(i)
+            if i + 2 < STEPS:
+                quant_x(i + 2)
+            if i + 1 < STEPS:
+                rope_sums(i + 1)
+                quant_latent(i + 1)
+            if i + 4 < STEPS:
+                cast(i + 4, "gg")
+            store(i)

@@ -40,6 +40,8 @@ def tile_llamaattention_pb_t_kernel(
 
         ident = const.tile([P, P], F32)
         make_identity(nc, ident[:])
+        ident_bf = const.tile([P, P], BF16)
+        nc.vector.tensor_copy(out=ident_bf[:], in_=ident[:])
 
         xb = []
         for g in range(8):
@@ -54,7 +56,8 @@ def tile_llamaattention_pb_t_kernel(
 
         nc.sync.dma_start(out=xb[0][:, 0:2, :], in_=x_view[0, 0][:, 0:2, :])
         nc.sync.dma_start(out=scale[:], in_=x_scale.rearrange("a o (p t) -> (a o p) t", t=4))
-        nc.sync.dma_start(out=wd_raw[:], in_=w_kv_d.rearrange("(p j) c -> p j c", j=4))
+        for c in (slice(0, 256), slice(256, 512)):
+            nc.sync.dma_start(out=wd_raw[:, :, c], in_=w_kv_d.rearrange("(p j) c -> p j c", j=4)[:, :, c])
         nc.sync.dma_start(out=xb[0][:, 2:4, :], in_=x_view[0, 0][:, 2:4, :])
         nc.sync.dma_start(out=wr_raw[:], in_=w_rope.rearrange("(p j) c -> p j c", j=4))
         nc.sync.dma_start(out=rot[:], in_=rotary.rearrange("a o (g p j) f -> (a o p) g j f", p=P, j=4))
@@ -68,15 +71,22 @@ def tile_llamaattention_pb_t_kernel(
         banks = {}
         prod, kt, vt = {}, {}, {}
 
-        def cast(s, engines):
-            wide = stage.tile([P, 2, 512], BF16, bufs=5, name="wide")
-            for a in range(2):
-                src = xb[s // 2][:, 2 * (s % 2) + a, :].bitcast(FP8)
-                if engines[a] == "v":
-                    nc.vector.tensor_copy(out=wide[:, a, :], in_=src)
-                else:
-                    nc.gpsimd.tensor_copy(out=wide[:, a, :], in_=src)
+        def cast(s, sides):
+            wide = stage.tile([P, 2, 512], BF16, bufs=4, name="wide")
             xw[s] = wide
+            j = 2 * (s % 2)
+            if sides == "v":
+                nc.vector.tensor_copy(
+                    out=wide[:].rearrange("p a k -> p (a k)"),
+                    in_=xb[s // 2][:, j : j + 2, :].rearrange("p a k -> p (a k)").bitcast(FP8),
+                )
+            else:
+                for a in range(2):
+                    src = xb[s // 2][:, j + a, :].bitcast(FP8)
+                    if sides[a] == "v":
+                        nc.vector.tensor_copy(out=wide[:, a, :], in_=src)
+                    else:
+                        nc.scalar.copy(out=wide[:, a, :], in_=src)
 
         def transposes(s):
             bank = psum.tile([P, 512], F32, name="bank")
@@ -130,7 +140,11 @@ def tile_llamaattention_pb_t_kernel(
             grouped = stage.tile([P, 2, P, 4], BF16, align_bytes=64, name="kgrouped")
             for a in range(2):
                 bank = banks.pop(("d", s, a))
-                nc.scalar.copy(out=grouped[:, a], in_=bank[:].rearrange("p (t m) -> p m t", t=4))
+                src = bank[:].rearrange("p (t m) -> p m t", t=4)
+                if s == STEPS - 1 and a == 1:
+                    nc.vector.tensor_copy(out=grouped[:, a], in_=src)
+                else:
+                    nc.scalar.copy(out=grouped[:, a], in_=src)
             kg[s] = grouped
 
         def quant_latent(s):
@@ -163,12 +177,21 @@ def tile_llamaattention_pb_t_kernel(
 
         def rope_sums(s):
             p = prod.pop(s)
-            nc.vector.tensor_tensor(
-                out=kt[s][:, :, :, ROT:HD].rearrange("p a h (c f) -> p c (a h) f", c=2),
-                in0=p[:, 0].rearrange("p a h f -> p (a h) f").unsqueeze(1).broadcast_to([P, 2, 2 * H, HALF]),
-                in1=p[:, 1:3].rearrange("p c a h f -> p c (a h) f"),
-                op=ADD,
-            )
+            if s == STEPS - 1:
+                nc.vector.tensor_tensor(
+                    out=kt[s][:, :, :, ROT:HD].rearrange("p a h (c f) -> p c (a h) f", c=2),
+                    in0=p[:, 0].rearrange("p a h f -> p (a h) f").unsqueeze(1).broadcast_to([P, 2, 2 * H, HALF]),
+                    in1=p[:, 1:3].rearrange("p c a h f -> p c (a h) f"),
+                    op=ADD,
+                )
+                return
+            for a in range(2):
+                nc.gpsimd.tensor_tensor(
+                    out=kt[s][:, a, :, ROT:HD].rearrange("p h (c f) -> p c h f", c=2),
+                    in0=p[:, 0, a].unsqueeze(1).broadcast_to([P, 2, H, HALF]),
+                    in1=p[:, 1:3, a],
+                    op=ADD,
+                )
 
         def values(s):
             codes, scales = kq.pop(s), ks.pop(s)
@@ -183,87 +206,126 @@ def tile_llamaattention_pb_t_kernel(
 
         def value_copies(s):
             vals = outs.tile([P, 2, 512], F32, name="vals")
-            for a in range(2):
-                nc.scalar.copy(out=vals[:, a, :], in_=banks.pop(("v", s, a))[:])
-            nc.scalar.copy(
-                out=kt[s][:, :, :, 0:ROT].rearrange("p a h d -> p (a h) d"),
-                in_=banks.pop(("c", s))[:].rearrange("p (q d) -> p q d", d=ROT),
-            )
+            last = s == STEPS - 1
+            nc.scalar.copy(out=vals[:, 0, :], in_=banks.pop(("v", s, 0))[:])
+            v1 = banks.pop(("v", s, 1))
+            if last:
+                nc.vector.tensor_copy(out=vals[:, 1, :], in_=v1[:])
+            else:
+                nc.scalar.copy(out=vals[:, 1, :], in_=v1[:])
+            key_out = kt[s][:, :, :, 0:ROT].rearrange("p a h d -> p (a h) d")
+            key_in = banks.pop(("c", s))[:].rearrange("p (q d) -> p q d", d=ROT)
+            if last:
+                nc.scalar.copy(out=key_out[:, 0:4], in_=key_in[:, 0:4])
+                nc.vector.tensor_copy(out=key_out[:, 4:8], in_=key_in[:, 4:8])
+            else:
+                nc.scalar.copy(out=key_out, in_=key_in)
             vt[s] = vals
 
         def store(s):
             b, g, j = s // 8, (s // 2) % 4, 2 * (s % 2)
-            nc.sync.dma_start(out=v_view[b, g][:, j : j + 2, :], in_=vt.pop(s)[:])
-            nc.sync.dma_start(out=k_view[b, g][:, j : j + 2, :], in_=kt.pop(s)[:].rearrange("p a h d -> p a (h d)"))
+            vals, keys = vt.pop(s), kt.pop(s)
+            pieces = 2 if s == STEPS - 1 else 1
+            n = 2 // pieces
+            for a in range(0, 2, n):
+                nc.sync.dma_start(out=v_view[b, g][:, j + a : j + a + n, :], in_=vals[:, a : a + n])
+                nc.sync.dma_start(
+                    out=k_view[b, g][:, j + a : j + a + n, :], in_=keys[:, a : a + n].rearrange("p a h d -> p a (h d)")
+                )
 
-        cast(0, "vv")
-        cast(1, "gg")
         wd_g = const.tile([P, 4, P, 4], BF16, align_bytes=64)
-        wd_in = wd_raw[:].rearrange("p j (m t) -> p t m j", t=4)
-        wr_g = const.tile([P, 2, H, HALF, 4], BF16, align_bytes=64)
-        wr_in = wr_raw[:].rearrange("p j (h c f) -> p c h f j", h=H, c=2)
-        wk_g = const.tile([P, 256, 4], BF16, align_bytes=64)
-        wv_g = const.tile([P, 512, 4], BF16, align_bytes=64)
-        wv_in = wv_raw[:].rearrange("p j c -> p c j")
+        wr_g = const.tile([P, 2, 4 * P], BF16, align_bytes=64)
+        wk_g = const.tile([P, 4 * 256], BF16, align_bytes=64)
+        wv_g = const.tile([P, 4 * 512], BF16, align_bytes=64)
         table = const.tile([P, 16, 3, HALF], F32)
         rot_in = rot[:].rearrange("p g j f -> p (g j) f")
 
+        def spread(raw):
+            bank = psum.tile([P, 512], F32, name="bank")
+            planes = bank[:].bitcast(BF16).rearrange("p (j c) -> p j c", j=4)
+            for j in range(0, 4, 2):
+                nc.tensor.matmul(planes[:, j : j + 2, :], lhsT=ident_bf[:], rhs=raw[:, j : j + 2, :], start=True, stop=True)
+            return planes
+
         def tables(lo, hi):
             sin, cos = rot_in[:, lo:hi, 0:HALF], rot_in[:, lo:hi, HALF:ROT]
-            nc.gpsimd.tensor_scalar(out=table[:, lo:hi, 0, :], in0=cos, scalar1=1.0, scalar2=0.0, op0=MULT, op1=ADD)
-            nc.gpsimd.tensor_scalar(out=table[:, lo:hi, 1, :], in0=cos, scalar1=-1.0, scalar2=0.0, op0=MULT, op1=ADD)
-            nc.gpsimd.tensor_tensor(out=table[:, lo:hi, 2, :], in0=sin, in1=cos, op=SUB)
-            nc.gpsimd.tensor_tensor(out=table[:, lo:hi, 1, :], in0=table[:, lo:hi, 1, :], in1=sin, op=SUB)
+            nc.vector.tensor_tensor(out=table[:, lo:hi, 2, :], in0=sin, in1=cos, op=SUB)
+            nc.vector.scalar_tensor_tensor(
+                out=table[:, lo:hi, 1, :], in0=cos, scalar=-1.0, in1=sin, op0=MULT, op1=SUB
+            )
 
+        def cos_tables(lo, hi):
+            nc.scalar.copy(out=table[:, lo:hi, 0, :], in_=rot_in[:, lo:hi, HALF:ROT])
+
+        cast(0, "vv")
         transposes(0)
+        planes = [spread(wd_raw[:, :, 256 * u : 256 * (u + 1)]) for u in range(2)]
+        for u in range(2):
+            nc.scalar.copy(
+                out=wd_g[:, :, 64 * u : 64 * (u + 1), :], in_=planes[u].rearrange("p j (m t) -> p t m j", t=4)
+            )
         scaled(0)
-        nc.scalar.copy(out=wd_g[:, 2:4], in_=wd_in[:, 2:4])
-        nc.vector.tensor_copy(out=wd_g[:, 0:2], in_=wd_in[:, 0:2])
+        cast(1, "v")
         quant_x(0)
-        tables(0, 4)
+        planes = spread(wr_raw[:])
         for c in range(2):
-            nc.scalar.copy(out=wr_g[:, c], in_=wr_in[:, 1 - c])
-        wd_q, wd_s = quantize(wd_g[:].rearrange("p t m j -> p (t m j)"), 512, const, "wd", 1)
-        nc.gpsimd.tensor_scalar(
-            out=wk_g[:], in0=wk_raw[:].rearrange("p j c -> p c j"), scalar1=1.0, scalar2=0.0, op0=MULT, op1=ADD
-        )
-        cast(2, "gg")
-
+            nc.scalar.copy(
+                out=wr_g[:, c].rearrange("p (h f j) -> p h f j", h=H, j=4),
+                in_=planes.rearrange("p j (h c f) -> p c h f j", h=H, c=2)[:, 1 - c],
+            )
         transposes(1)
-        latents(0)
+        wd_q, wd_s = quantize(wd_g[:].rearrange("p t m j -> p (t m j)"), 512, const, "wd", 1)
         scaled(1)
-        wr_q, wr_s = quantize(wr_g[:].rearrange("p c h f j -> p (c h f j)"), 256, const, "wr", 1)
+        planes = spread(wk_raw[:])
+        nc.scalar.copy(out=wk_g[:].rearrange("p (c j) -> p c j", j=4), in_=planes.rearrange("p j c -> p c j"))
+        cos_tables(0, 4)
+        wr_q, wr_s = quantize(wr_g[:].rearrange("p c n -> p (c n)"), 256, const, "wr", 1)
+        latents(0)
         rope_matmuls(0)
         latent_copies(0)
+        tables(0, 4)
         quant_x(1)
-        nc.vector.tensor_copy(out=wv_g[:, 0:256], in_=wv_in[:, 0:256])
-        nc.scalar.copy(out=wv_g[:, 256:512], in_=wv_in[:, 256:512])
+        cast(2, "v")
+        planes = [spread(wv_raw[:, :, 256 * u : 256 * (u + 1)]) for u in range(2)]
+        for u in range(2):
+            nc.scalar.copy(
+                out=wv_g[:, 1024 * u : 1024 * (u + 1)].rearrange("p (c j) -> p c j", j=4),
+                in_=planes[u].rearrange("p j c -> p c j"),
+            )
         quant_latent(0)
-        wk_q, wk_s = quantize(wk_g[:].rearrange("p c j -> p (c j)"), 256, const, "wk", 1)
+        wk_q, wk_s = quantize(wk_g[:], 256, const, "wk", 1)
         rope_products(0)
-        wv_q, wv_s = quantize(wv_g[:].rearrange("p c j -> p (c j)"), 512, const, "wv", 1)
         rope_sums(0)
-        cast(3, "gg")
-        tables(4, 16)
+        transposes(2)
+        scaled(2)
+        wv_q, wv_s = quantize(wv_g[:], 512, const, "wv", 1)
 
         for i in range(STEPS):
-            if i + 2 < STEPS:
+            split = i % 2 == 1 and i + 3 < STEPS
+            if 0 < i and i + 2 < STEPS:
                 transposes(i + 2)
             if i + 1 < STEPS:
                 latents(i + 1)
                 rope_matmuls(i + 1)
             values(i)
-            if i + 2 < STEPS:
+            if 0 < i and i + 2 < STEPS:
                 scaled(i + 2)
+            if i + 3 < STEPS:
+                cast(i + 3, "vs" if split else "v")
+            if i in (0, 2, 4):
+                cos_tables(2 * i + 4, 2 * i + 8)
+                tables(2 * i + 4, 2 * i + 8)
+            if i + 2 == STEPS:
+                rope_products(i + 1)
             if i + 1 < STEPS:
                 latent_copies(i + 1)
-                rope_products(i + 1)
-            value_copies(i)
             if i + 2 < STEPS:
                 quant_x(i + 2)
             if i + 1 < STEPS:
-                rope_sums(i + 1)
                 quant_latent(i + 1)
-            if i + 4 < STEPS:
-                cast(i + 4, "gg")
+            if i + 2 < STEPS:
+                rope_products(i + 1)
+            if i + 1 < STEPS:
+                rope_sums(i + 1)
+            value_copies(i)
             store(i)

from contextlib import ExitStack

import concourse.mybir as mybir
from concourse.masks import make_identity

F32 = mybir.dt.float32
BF16 = mybir.dt.bfloat16
U32 = mybir.dt.uint32
U8 = mybir.dt.uint8
FP8 = mybir.dt.float8_e4m3fn
FP8X4 = mybir.dt.float8_e4m3fn_x4
MULT = mybir.AluOpType.mult
ADD = mybir.AluOpType.add
SUB = mybir.AluOpType.subtract

P = 128
B, S, HID, LAT = 2, 2048, 512, 512
H, HD, ROT, HALF = 4, 128, 64, 32
GROUP = 4 * P
STEP = 2 * P
STEPS = B * S // STEP

FLOPS = 2 * B * S * 512 * (512 + 256 + 512 + 256)


def tile_llamaattention_pb_t_kernel(
    tc, x_bytes, x_scale, rotary, w_kv_d, w_k_u, w_v_u, w_rope, k_out, v_out
):
    nc = tc.nc
    x_view = x_bytes.rearrange("b (g p j) k -> b g p j k", p=P, j=4)
    k_view = k_out.rearrange("b (g p j) h d -> b g p j (h d)", p=P, j=4)
    v_view = v_out.rearrange("b (g p j) h d -> b g p j (h d)", p=P, j=4)

    with ExitStack() as ctx:
        const = ctx.enter_context(tc.tile_pool(name="const", bufs=1))
        stage = ctx.enter_context(tc.tile_pool(name="stage", bufs=3))
        outs = ctx.enter_context(tc.tile_pool(name="outs", bufs=4))
        psum = ctx.enter_context(tc.psum_pool(name="psum", bufs=8))
        ctx.enter_context(tc.manual_schedule())

        ident = const.tile([P, P], F32)
        make_identity(nc, ident[:])
        ident_bf = const.tile([P, P], BF16)
        nc.vector.tensor_copy(out=ident_bf[:], in_=ident[:])

        xb = []
        for g in range(8):
            xbytes = const.tile([P, 4, 512], U8, name="xbytes%d" % g)
            xb.append(xbytes)
        scale = const.tile([P, 4], F32)
        wd_raw = const.tile([P, 4, 512], BF16)
        wr_raw = const.tile([P, 4, 256], BF16)
        wk_raw = const.tile([P, 4, 256], BF16)
        wv_raw = const.tile([P, 4, 512], BF16)
        rot = const.tile([P, 4, 4, ROT], BF16)

        nc.sync.dma_start(out=xb[0][:, 0:2, :], in_=x_view[0, 0][:, 0:2, :])
        nc.sync.dma_start(out=scale[:], in_=x_scale.rearrange("a o (p t) -> (a o p) t", t=4))
        for c in (slice(0, 256), slice(256, 512)):
            nc.sync.dma_start(out=wd_raw[:, :, c], in_=w_kv_d.rearrange("(p j) c -> p j c", j=4)[:, :, c])
        nc.sync.dma_start(out=xb[0][:, 2:4, :], in_=x_view[0, 0][:, 2:4, :])
        nc.sync.dma_start(out=wr_raw[:], in_=w_rope.rearrange("(p j) c -> p j c", j=4))
        nc.sync.dma_start(out=rot[:], in_=rotary.rearrange("a o (g p j) f -> (a o p) g j f", p=P, j=4))
        nc.sync.dma_start(out=wk_raw[:], in_=w_k_u.rearrange("(p j) c -> p j c", j=4))
        nc.sync.dma_start(out=wv_raw[:], in_=w_v_u.rearrange("(p j) c -> p j c", j=4))
        for g in range(1, 8):
            nc.sync.dma_start(out=xb[g][:], in_=x_view[g // 4, g % 4])

        xw, xg, xq, xs = {}, {}, {}, {}
        kg, kq, ks = {}, {}, {}
        banks = {}
        prod, kt, vt = {}, {}, {}

        def cast(s, sides):
            wide = stage.tile([P, 2, 512], BF16, bufs=4, name="wide")
            xw[s] = wide
            j = 2 * (s % 2)
            if sides == "v":
                nc.vector.tensor_copy(
                    out=wide[:].rearrange("p a k -> p (a k)"),
                    in_=xb[s // 2][:, j : j + 2, :].rearrange("p a k -> p (a k)").bitcast(FP8),
                )
            else:
                for a in range(2):
                    src = xb[s // 2][:, j + a, :].bitcast(FP8)
                    if sides[a] == "v":
                        nc.vector.tensor_copy(out=wide[:, a, :], in_=src)
                    else:
                        nc.scalar.copy(out=wide[:, a, :], in_=src)

        def transposes(s):
            bank = psum.tile([P, 512], F32, name="bank")
            halves = bank[:].rearrange("p (u a m) -> p u a m", u=2, a=2)
            words = xw.pop(s)[:].rearrange("p a k -> p (a k)").bitcast(F32)
            for a in range(2):
                for u in range(2):
                    nc.tensor.transpose(halves[:, u, a, :], words[:, 256 * a + u : 256 * (a + 1) : 2], ident[:])
            banks["t", s] = bank

        def scaled(s):
            bank = banks.pop(("t", s))
            grouped = stage.tile([P, STEP, 2, 2], BF16, align_bytes=64, name="xgrouped")
            nc.vector.tensor_tensor(
                out=grouped[:],
                in0=bank[:].bitcast(BF16).rearrange("p (u r e) -> p r u e", u=2, e=2),
                in1=scale[:].rearrange("p (u e) -> p u e", e=2).unsqueeze(1).broadcast_to([P, STEP, 2, 2]),
                op=MULT,
            )
            xg[s] = grouped

        def quantize(src, width, pool, label, bufs):
            codes = pool.tile([P, width], U32, align_bytes=64, bufs=bufs, name="%scodes" % label)
            scales = pool.tile([P, width], U8, align_bytes=64, bufs=bufs, name="%sscales" % label)
            nc.vector.quantize_mx(out=codes[:].bitcast(FP8X4), scales=scales[:], in_=src)
            return codes, scales

        def quant_x(s):
            xq[s], xs[s] = quantize(xg.pop(s)[:].rearrange("p r u e -> p (r u e)"), STEP, stage, "x", 3)

        def mm(out, lhs, lhs_s, lc, rhs, rhs_s, rc, start=True, stop=True):
            nc.tensor.matmul_mx(
                out=out,
                lhsT=lhs[:, lc].bitcast(FP8X4),
                lhsT_scale=lhs_s[:, lc],
                rhs=rhs[:, rc].bitcast(FP8X4),
                rhs_scale=rhs_s[:, rc],
                start=start,
                stop=stop,
            )

        def latents(s):
            for a in range(2):
                bank = psum.tile([P, 512], F32, name="bank")
                for t in range(4):
                    cols = slice(128 * t, 128 * (t + 1))
                    mm(bank[:, cols], wd_q, wd_s, cols, xq[s], xs[s], slice(128 * a, 128 * (a + 1)))
                banks["d", s, a] = bank

        def latent_copies(s):
            grouped = stage.tile([P, 2, P, 4], BF16, align_bytes=64, name="kgrouped")
            for a in range(2):
                bank = banks.pop(("d", s, a))
                src = bank[:].rearrange("p (t m) -> p m t", t=4)
                if s == STEPS - 1 and a == 1:
                    nc.vector.tensor_copy(out=grouped[:, a], in_=src)
                else:
                    nc.scalar.copy(out=grouped[:, a], in_=src)
            kg[s] = grouped

        def quant_latent(s):
            kq[s], ks[s] = quantize(kg.pop(s)[:].rearrange("p a m t -> p (a m t)"), STEP, stage, "k", 3)

        def rope_matmuls(s):
            codes, scales = xq.pop(s), xs.pop(s)
            for a in range(2):
                bank = psum.tile([P, 512], F32, name="bank")
                rows = slice(128 * a, 128 * (a + 1))
                mm(bank[:, 0:128], codes, scales, rows, wr_q, wr_s, slice(0, 128), True, False)
                mm(bank[:, 0:128], codes, scales, rows, wr_q, wr_s, slice(128, 256), False, True)
                mm(bank[:, 128:384], codes, scales, rows, wr_q, wr_s, slice(0, 256))
                banks["r", s, a] = bank

        def rope_products(s):
            p = stage.tile([P, 3, 2, H, HALF], F32, name="products")
            for a in range(2):
                slab = (2 * s + a) % 16
                bank = banks.pop(("r", s, a))
                nc.vector.tensor_tensor(
                    out=p[:, :, a],
                    in0=bank[:, 0:384].rearrange("p (c h f) -> p c h f", c=3, h=H),
                    in1=table[:, slab].unsqueeze(2).broadcast_to([P, 3, H, HALF]),
                    op=MULT,
                )
            prod[s] = p
            keys = outs.tile([P, 2, H, HD], F32, name="keys")
            kt[s] = keys

        def rope_sums(s):
            p = prod.pop(s)
            if s == STEPS - 1:
                nc.vector.tensor_tensor(
                    out=kt[s][:, :, :, ROT:HD].rearrange("p a h (c f) -> p c (a h) f", c=2),
                    in0=p[:, 0].rearrange("p a h f -> p (a h) f").unsqueeze(1).broadcast_to([P, 2, 2 * H, HALF]),
                    in1=p[:, 1:3].rearrange("p c a h f -> p c (a h) f"),
                    op=ADD,
                )
                return
            for a in range(2):
                nc.gpsimd.tensor_tensor(
                    out=kt[s][:, a, :, ROT:HD].rearrange("p h (c f) -> p c h f", c=2),
                    in0=p[:, 0, a].unsqueeze(1).broadcast_to([P, 2, H, HALF]),
                    in1=p[:, 1:3, a],
                    op=ADD,
                )

        def values(s):
            codes, scales = kq.pop(s), ks.pop(s)
            for a in range(2):
                bank = psum.tile([P, 512], F32, name="bank")
                mm(bank[:], codes, scales, slice(128 * a, 128 * (a + 1)), wv_q, wv_s, slice(0, 512))
                banks["v", s, a] = bank
            bank = psum.tile([P, 512], F32, name="bank")
            for a in range(2):
                mm(bank[:, 256 * a : 256 * (a + 1)], codes, scales, slice(128 * a, 128 * (a + 1)), wk_q, wk_s, slice(0, 256))
            banks["c", s] = bank

        def value_copies(s):
            vals = outs.tile([P, 2, 512], F32, name="vals")
            last = s == STEPS - 1
            nc.scalar.copy(out=vals[:, 0, :], in_=banks.pop(("v", s, 0))[:])
            v1 = banks.pop(("v", s, 1))
            if last:
                nc.vector.tensor_copy(out=vals[:, 1, :], in_=v1[:])
            else:
                nc.scalar.copy(out=vals[:, 1, :], in_=v1[:])
            key_out = kt[s][:, :, :, 0:ROT].rearrange("p a h d -> p (a h) d")
            key_in = banks.pop(("c", s))[:].rearrange("p (q d) -> p q d", d=ROT)
            if last:
                nc.scalar.copy(out=key_out[:, 0:4], in_=key_in[:, 0:4])
                nc.vector.tensor_copy(out=key_out[:, 4:8], in_=key_in[:, 4:8])
            else:
                nc.scalar.copy(out=key_out, in_=key_in)
            vt[s] = vals

        def store(s):
            b, g, j = s // 8, (s // 2) % 4, 2 * (s % 2)
            vals, keys = vt.pop(s), kt.pop(s)
            pieces = 2 if s == STEPS - 1 else 1
            n = 2 // pieces
            for a in range(0, 2, n):
                nc.sync.dma_start(out=v_view[b, g][:, j + a : j + a + n, :], in_=vals[:, a : a + n])
                nc.sync.dma_start(
                    out=k_view[b, g][:, j + a : j + a + n, :], in_=keys[:, a : a + n].rearrange("p a h d -> p a (h d)")
                )

        wd_g = const.tile([P, 4, P, 4], BF16, align_bytes=64)
        wr_g = const.tile([P, 2, 4 * P], BF16, align_bytes=64)
        wk_g = const.tile([P, 4 * 256], BF16, align_bytes=64)
        wv_g = const.tile([P, 4 * 512], BF16, align_bytes=64)
        table = const.tile([P, 16, 3, HALF], F32)
        rot_in = rot[:].rearrange("p g j f -> p (g j) f")

        def spread(raw):
            bank = psum.tile([P, 512], F32, name="bank")
            planes = bank[:].bitcast(BF16).rearrange("p (j c) -> p j c", j=4)
            for j in range(0, 4, 2):
                nc.tensor.matmul(planes[:, j : j + 2, :], lhsT=ident_bf[:], rhs=raw[:, j : j + 2, :], start=True, stop=True)
            return planes

        def tables(lo, hi):
            sin, cos = rot_in[:, lo:hi, 0:HALF], rot_in[:, lo:hi, HALF:ROT]
            nc.vector.tensor_tensor(out=table[:, lo:hi, 2, :], in0=sin, in1=cos, op=SUB)
            nc.vector.scalar_tensor_tensor(
                out=table[:, lo:hi, 1, :], in0=cos, scalar=-1.0, in1=sin, op0=MULT, op1=SUB
            )

        def cos_tables(lo, hi):
            nc.scalar.copy(out=table[:, lo:hi, 0, :], in_=rot_in[:, lo:hi, HALF:ROT])

        cast(0, "vv")
        transposes(0)
        planes = [spread(wd_raw[:, :, 256 * u : 256 * (u + 1)]) for u in range(2)]
        for u in range(2):
            nc.scalar.copy(
                out=wd_g[:, :, 64 * u : 64 * (u + 1), :], in_=planes[u].rearrange("p j (m t) -> p t m j", t=4)
            )
        scaled(0)
        cast(1, "v")
        quant_x(0)
        planes = spread(wr_raw[:])
        for c in range(2):
            nc.scalar.copy(
                out=wr_g[:, c].rearrange("p (h f j) -> p h f j", h=H, j=4),
                in_=planes.rearrange("p j (h c f) -> p c h f j", h=H, c=2)[:, 1 - c],
            )
        transposes(1)
        wd_q, wd_s = quantize(wd_g[:].rearrange("p t m j -> p (t m j)"), 512, const, "wd", 1)
        scaled(1)
        planes = spread(wk_raw[:])
        nc.scalar.copy(out=wk_g[:].rearrange("p (c j) -> p c j", j=4), in_=planes.rearrange("p j c -> p c j"))
        cos_tables(0, 4)
        wr_q, wr_s = quantize(wr_g[:].rearrange("p c n -> p (c n)"), 256, const, "wr", 1)
        latents(0)
        rope_matmuls(0)
        latent_copies(0)
        tables(0, 4)
        quant_x(1)
        cast(2, "v")
        planes = [spread(wv_raw[:, :, 256 * u : 256 * (u + 1)]) for u in range(2)]
        for u in range(2):
            nc.scalar.copy(
                out=wv_g[:, 1024 * u : 1024 * (u + 1)].rearrange("p (c j) -> p c j", j=4),
                in_=planes[u].rearrange("p j c -> p c j"),
            )
        quant_latent(0)
        wk_q, wk_s = quantize(wk_g[:], 256, const, "wk", 1)
        rope_products(0)
        rope_sums(0)
        transposes(2)
        scaled(2)
        wv_q, wv_s = quantize(wv_g[:], 512, const, "wv", 1)

        for i in range(STEPS):
            split = i % 2 == 1 and i + 3 < STEPS
            if 0 < i and i + 2 < STEPS:
                transposes(i + 2)
            if i + 1 < STEPS:
                latents(i + 1)
                rope_matmuls(i + 1)
            values(i)
            if 0 < i and i + 2 < STEPS:
                scaled(i + 2)
            if i + 3 < STEPS:
                cast(i + 3, "vs" if split else "v")
            if i in (0, 2, 4):
                cos_tables(2 * i + 4, 2 * i + 8)
                tables(2 * i + 4, 2 * i + 8)
            if i + 2 == STEPS:
                rope_products(i + 1)
            if i + 1 < STEPS:
                latent_copies(i + 1)
            if i + 2 < STEPS:
                quant_x(i + 2)
            if i + 1 < STEPS:
                quant_latent(i + 1)
            if i + 2 < STEPS:
                rope_products(i + 1)
            if i + 1 < STEPS:
                rope_sums(i + 1)
            value_copies(i)
            store(i)
